import numpy as np
import ml_dtypes


def mxq(x, axis, fmt="e4m3"):
    dtype, down = {"e4m3": (ml_dtypes.float8_e4m3fn, 7), "e5m2": (ml_dtypes.float8_e5m2, 14)}[fmt]
    v = np.moveaxis(np.asarray(x, np.float32).astype(ml_dtypes.bfloat16).astype(np.float64), axis, -1)
    blocks = v.reshape(v.shape[:-1] + (-1, 32))
    amax = np.abs(blocks).max(-1, keepdims=True)
    byte = np.maximum(np.where(amax > 0, np.frexp(amax)[1] - 1 + 127, 0) - down, 1)
    scale = np.exp2(byte - 127.0)
    codes = (blocks / scale).astype(np.float32).astype(dtype).astype(np.float64)
    return np.moveaxis((codes * scale).reshape(v.shape), -1, axis)


WIDE = False


def mx_kscale(k):
    if not WIDE:
        return np.ones(k)
    levels = np.array([10, -10, 5, -5, 0])
    if k % 512:
        return np.exp2(np.random.permutation(np.resize(levels, k // 32))).repeat(32)
    a = np.empty((k // 512, 16))
    for p in range(k // 512):
        a[p, :8] = np.random.permutation(np.resize(levels, 8))
        for g in range(8):
            far = levels[np.abs(levels - a[p, g]) >= 10]
            a[p, g + 8] = far[np.random.randint(len(far))]
    return np.exp2(a.ravel()).repeat(32)


BF16 = ml_dtypes.bfloat16


def bf(x):
    return np.asarray(x, np.float32).astype(BF16)


def f64(x):
    return np.asarray(x).astype(np.float64)


B, HH, WW, E, NH, D = 1, 512, 4, 1024, 8, 128
KD = NH * D


def setup_inputs():
    t = mx_kscale(KD)
    return {"ret_w": bf(np.random.standard_normal((B, HH, WW, NH, D)) * 0.9),
            "kv_h": bf(np.random.standard_normal((B, WW, NH, D, D)) * 0.8 * t.reshape(NH, 1, D)),
            "Wo": bf(np.random.standard_normal((E, KD)) * 0.3 / np.sqrt(KD) / t),
            "bo": bf(np.random.standard_normal(E) * 0.2)}


def reference(ret_w, kv_h, Wo, bo):
    o = f64(ret_w).reshape(B, HH, WW * NH, D).transpose(0, 2, 1, 3) @ f64(kv_h).reshape(B, WW * NH, D, D)
    o = o.transpose(0, 2, 1, 3).reshape(B, HH, WW, KD)
    y = (mxq(o, 3, "e4m3") @ mxq(f64(Wo).T, 0, "e4m3")) + f64(bo)
    return y.reshape(B, HH * WW, E)

@@ -1,0 +1,218 @@
+from contextlib import ExitStack
+
+import concourse.mybir as mybir
+from concourse.masks import make_identity
+
+BF16 = mybir.dt.bfloat16
+F32 = mybir.dt.float32
+U32 = mybir.dt.uint32
+U8 = mybir.dt.uint8
+FP8X4 = mybir.dt.float8_e4m3fn_x4
+
+P = 128
+HEIGHT, WIDTH, HEADS, HEAD_DIM, OUT_CH = 512, 4, 8, 128, 1024
+CHANNELS = HEADS * HEAD_DIM
+PACK = 4
+PASSES = CHANNELS // (P * PACK)
+PAIR = 2
+WORDS = PACK // PAIR
+H_BLOCKS = HEIGHT // P
+UNITS = WIDTH * H_BLOCKS
+N_TILE = 512
+COL_HALVES = OUT_CH // N_TILE
+WO_BLOCKS = OUT_CH // P
+HALF_BLOCKS = N_TILE // P
+MX_LAG = 4
+
+FLOPS = 2 * HEIGHT * WIDTH * CHANNELS * HEAD_DIM + 2 * HEIGHT * WIDTH * CHANNELS * OUT_CH
+
+
+def tile_linear_retention_pb_kernel(tc, ret_w, kv_h, Wo, bo, out):
+    nc = tc.nc
+
+    x_dram = ret_w[0].rearrange("(hb h) w n e -> w hb h (n e)", h=P)
+    kv_dram = kv_h[0].rearrange("w n e f -> w e n f")
+    wo_dram = Wo.rearrange("(cb c) k -> c cb k", c=P)
+    out_dram = out[0].rearrange("(hb h w) c -> w hb h c", h=P, w=WIDTH)
+
+    with ExitStack() as ctx:
+        keep = ctx.enter_context(tc.tile_pool(name="keep", bufs=1))
+        work = ctx.enter_context(tc.tile_pool(name="work", bufs=3))
+        quantised = ctx.enter_context(tc.tile_pool(name="quantised", bufs=3))
+        results = ctx.enter_context(tc.tile_pool(name="results", bufs=8))
+        psum_x = ctx.enter_context(tc.psum_pool(name="psum_x", bufs=2))
+        psum_o = ctx.enter_context(tc.psum_pool(name="psum_o", bufs=2))
+        psum_w = ctx.enter_context(tc.psum_pool(name="psum_w", bufs=2))
+        psum_y = ctx.enter_context(tc.psum_pool(name="psum_y", bufs=COL_HALVES))
+        ctx.enter_context(tc.manual_schedule())
+
+        bias_rows = keep.tile([P, OUT_CH], BF16)
+        nc.vector.memset(bias_rows[:], 0.0)
+        ones = keep.tile([P, P], BF16)
+        nc.vector.memset(ones[:], 1.0)
+        ident = keep.tile([P, P], BF16)
+        make_identity(nc, ident[:])
+        ident_words = keep.tile([P, P], F32)
+        make_identity(nc, ident_words[:])
+
+        x_sb = keep.tile([P, UNITS, CHANNELS], BF16)
+        kv_sb = keep.tile([P, WIDTH, HEADS, HEAD_DIM], BF16)
+        wo_sb = keep.tile([P, WO_BLOCKS, CHANNELS], BF16)
+        for u in range(UNITS):
+            w, hb = divmod(u, H_BLOCKS)
+            nc.sync.dma_start(out=x_sb[:, u, :], in_=x_dram[w, hb])
+            if hb == 0:
+                nc.sync.dma_start(out=kv_sb[:, w], in_=kv_dram[w])
+            if u == 0:
+                nc.sync.dma_start(out=bias_rows[0:1, :], in_=bo.rearrange("(o c) -> o c", o=1))
+            if 0 <= u - 1 < COL_HALVES:
+                for cb in range((u - 1) * HALF_BLOCKS, u * HALF_BLOCKS):
+                    nc.sync.dma_start(out=wo_sb[:, cb, :], in_=wo_dram[:, cb, :])
+
+        bias = keep.tile([P, OUT_CH], F32)
+
+        def spread_bias():
+            for ch in range(COL_HALVES):
+                cols = slice(ch * N_TILE, (ch + 1) * N_TILE)
+                spread = psum_y.tile([P, N_TILE], F32, tag="y_ps")
+                nc.tensor.matmul(out=spread[:], lhsT=ones[:], rhs=bias_rows[:, cols], start=True, stop=True)
+                nc.vector.tensor_copy(out=bias[:, cols], in_=spread[:])
+
+        wo_grouped = keep.tile([P, PASSES, OUT_CH, PACK], BF16, align_bytes=64)
+        wo_grouped_words = wo_grouped[:].rearrange("p g c t -> p (g c t)").bitcast(F32).rearrange(
+            "p (g c u) -> p g c u", g=PASSES, u=WORDS
+        )
+        wo_codes = keep.tile([P, PASSES, OUT_CH], U32, align_bytes=64)
+        wo_scales = keep.tile([P, PASSES, OUT_CH], U8, align_bytes=64)
+
+        def transpose_wo_block(cb):
+            words = wo_sb[:, cb, :].bitcast(F32)
+            wo_t = psum_w.tile([P, PASSES, WORDS, P], F32, tag="w_ps")
+            for g in range(PASSES):
+                for u in range(WORDS):
+                    first = g * P * WORDS + u
+                    nc.tensor.transpose(
+                        out=wo_t[:, g, u, :],
+                        in_=words[:, first : first + P * WORDS - u : WORDS],
+                        identity=ident_words[:],
+                    )
+            grouped_block = wo_grouped_words[:, :, cb * P : (cb + 1) * P, :]
+            hopping = wo_t[:].rearrange("p g u c -> p g c u")
+            if cb % 2 == 0:
+                nc.vector.tensor_copy(out=grouped_block, in_=hopping)
+            else:
+                nc.scalar.copy(out=grouped_block, in_=hopping)
+
+        def quantise_wo_half(ch):
+            cols = slice(ch * N_TILE, (ch + 1) * N_TILE)
+            for g in range(PASSES):
+                nc.vector.quantize_mx(
+                    out=wo_codes[:, g, cols].bitcast(FP8X4),
+                    scales=wo_scales[:, g, cols],
+                    in_=wo_grouped[:, g, cols, :].rearrange("p c t -> p (c t)"),
+                )
+
+        x_t = {}
+        o_rows = {}
+        o_grouped = {}
+        o_codes = {}
+        o_scales = {}
+
+        def transpose_unit(u):
+            x_t_ps = psum_x.tile([P, HEADS, P], BF16, tag="x_ps")
+            for n in range(HEADS):
+                nc.tensor.transpose(
+                    out=x_t_ps[:, n, :], in_=x_sb[:, u, n * P : (n + 1) * P], identity=ident[:]
+                )
+            x_t_sb = work.tile([P, HEADS, P], BF16, tag="x_t")
+            nc.scalar.copy(out=x_t_sb[:], in_=x_t_ps[:])
+            x_t[u] = x_t_sb
+
+        def read_out(u, g):
+            w = u // H_BLOCKS
+            if g == 0:
+                rows = work.tile([P, PASSES, WORDS, P, PAIR], BF16, tag="o_rows")
+                o_rows[u] = rows
+            o_ps = psum_o.tile([P, PACK * P], F32, tag="o_ps")
+            for t in range(PACK):
+                n = g * PACK + t
+                nc.tensor.matmul(
+                    out=o_ps[:, t * P : (t + 1) * P],
+                    lhsT=x_t[u][:, n, :],
+                    rhs=kv_sb[:, w, n, :],
+                    start=True,
+                    stop=True,
+                )
+            nc.scalar.copy(
+                out=o_rows[u][:, g],
+                in_=o_ps[:].rearrange("h (p u e) -> h u p e", u=WORDS, e=PAIR),
+            )
+
+        def transpose_back(u):
+            words = o_rows[u][:].rearrange("h g u p e -> h (g u p e)").bitcast(F32)
+            o_t_ps = psum_w.tile([P, PASSES, WORDS, P], F32, tag="w_ps")
+            for g in range(PASSES):
+                for v in range(WORDS):
+                    first = (g * WORDS + v) * P
+                    nc.tensor.transpose(
+                        out=o_t_ps[:, g, v, :], in_=words[:, first : first + P], identity=ident_words[:]
+                    )
+            grouped = work.tile([P, PASSES, P, PACK], BF16, tag="o_grouped", align_bytes=64)
+            nc.vector.tensor_copy(
+                out=grouped[:].rearrange("p g h t -> p (g h t)").bitcast(F32).rearrange(
+                    "p (g h u) -> p g h u", g=PASSES, u=WORDS
+                ),
+                in_=o_t_ps[:].rearrange("p g u h -> p g h u"),
+            )
+            o_grouped[u] = grouped
+
+        def quantise_unit(u):
+            codes = quantised.tile([P, PASSES, P], U32, tag="o_codes", align_bytes=64)
+            scales = quantised.tile([P, PASSES, P], U8, tag="o_scales", align_bytes=64)
+            nc.vector.quantize_mx(
+                out=codes[:].rearrange("p g h -> p (g h)").bitcast(FP8X4),
+                scales=scales[:].rearrange("p g h -> p (g h)"),
+                in_=o_grouped[u][:].rearrange("p g h t -> p (g h t)"),
+            )
+            o_codes[u] = codes
+            o_scales[u] = scales
+
+        def project(u):
+            w, hb = divmod(u, H_BLOCKS)
+            for ch in range(COL_HALVES):
+                cols = slice(ch * N_TILE, (ch + 1) * N_TILE)
+                y_ps = psum_y.tile([P, N_TILE], F32, tag="y_ps")
+                for g in range(PASSES):
+                    nc.tensor.matmul_mx(
+                        out=y_ps[:],
+                        lhsT=o_codes[u][:, g, :].bitcast(FP8X4),
+                        lhsT_scale=o_scales[u][:, g, :],
+                        rhs=wo_codes[:, g, cols].bitcast(FP8X4),
+                        rhs_scale=wo_scales[:, g, cols],
+                        start=(g == 0),
+                        stop=(g == PASSES - 1),
+                    )
+                y = results.tile([P, N_TILE], F32, tag="y")
+                nc.vector.tensor_tensor(out=y[:], in0=y_ps[:], in1=bias[:, cols], op=mybir.AluOpType.add)
+                nc.sync.dma_start(out=out_dram[w, hb][:, cols], in_=y[:])
+
+        for i in range(UNITS + MX_LAG):
+            if 0 <= i - 3 < UNITS:
+                quantise_unit(i - 3)
+            if 0 <= i - 2 < COL_HALVES:
+                quantise_wo_half(i - 2)
+            if 0 <= i - 1 < UNITS:
+                read_out(i - 1, 0)
+            if i < UNITS:
+                transpose_unit(i)
+            if 0 <= i - 2 < UNITS:
+                transpose_back(i - 2)
+            if i == 0:
+                spread_bias()
+            if 0 <= i - 1 < COL_HALVES:
+                for cb in range((i - 1) * HALF_BLOCKS, i * HALF_BLOCKS):
+                    transpose_wo_block(cb)
+            if 0 <= i - 1 < UNITS:
+                read_out(i - 1, 1)
+            if i >= MX_LAG:
+                project(i - MX_LAG)

@@ -22,7 +22,10 @@ N_TILE = 512
 COL_HALVES = OUT_CH // N_TILE
 WO_BLOCKS = OUT_CH // P
 HALF_BLOCKS = N_TILE // P
-MX_LAG = 4
+WO_PER_ROUND = 2
+WO_ROUNDS = WO_BLOCKS // WO_PER_ROUND
+WARM_UP = 4
+MX_LAG = WO_ROUNDS + 2
 
 FLOPS = 2 * HEIGHT * WIDTH * CHANNELS * HEAD_DIM + 2 * HEIGHT * WIDTH * CHANNELS * OUT_CH
 
@@ -38,7 +41,7 @@ def tile_linear_retention_pb_kernel(tc, ret_w, kv_h, Wo, bo, out):
     with ExitStack() as ctx:
         keep = ctx.enter_context(tc.tile_pool(name="keep", bufs=1))
         work = ctx.enter_context(tc.tile_pool(name="work", bufs=3))
-        quantised = ctx.enter_context(tc.tile_pool(name="quantised", bufs=3))
+        quantised = ctx.enter_context(tc.tile_pool(name="quantised", bufs=MX_LAG - 1))
         results = ctx.enter_context(tc.tile_pool(name="results", bufs=8))
         psum_x = ctx.enter_context(tc.psum_pool(name="psum_x", bufs=2))
         psum_o = ctx.enter_context(tc.psum_pool(name="psum_o", bufs=2))
@@ -48,7 +51,7 @@ def tile_linear_retention_pb_kernel(tc, ret_w, kv_h, Wo, bo, out):
 
         bias_rows = keep.tile([P, OUT_CH], BF16)
         nc.vector.memset(bias_rows[:], 0.0)
-        ones = keep.tile([P, P], BF16)
+        ones = keep.tile([P, N_TILE], BF16)
         nc.vector.memset(ones[:], 1.0)
         ident = keep.tile([P, P], BF16)
         make_identity(nc, ident[:])
@@ -65,9 +68,13 @@ def tile_linear_retention_pb_kernel(tc, ret_w, kv_h, Wo, bo, out):
                 nc.sync.dma_start(out=kv_sb[:, w], in_=kv_dram[w])
             if u == 0:
                 nc.sync.dma_start(out=bias_rows[0:1, :], in_=bo.rearrange("(o c) -> o c", o=1))
-            if 0 <= u - 1 < COL_HALVES:
-                for cb in range((u - 1) * HALF_BLOCKS, u * HALF_BLOCKS):
+            if 1 <= u <= WO_ROUNDS:
+                for cb in range((u - 1) * WO_PER_ROUND, u * WO_PER_ROUND):
                     nc.sync.dma_start(out=wo_sb[:, cb, :], in_=wo_dram[:, cb, :])
+
+        def keep_warm():
+            unread = psum_y.tile([P, N_TILE], F32, tag="y_ps")
+            nc.tensor.matmul(out=unread[:], lhsT=ones[:, 0:P], rhs=ones[:], start=True, stop=True)
 
         bias = keep.tile([P, OUT_CH], F32)
 
@@ -75,7 +82,7 @@ def tile_linear_retention_pb_kernel(tc, ret_w, kv_h, Wo, bo, out):
             for ch in range(COL_HALVES):
                 cols = slice(ch * N_TILE, (ch + 1) * N_TILE)
                 spread = psum_y.tile([P, N_TILE], F32, tag="y_ps")
-                nc.tensor.matmul(out=spread[:], lhsT=ones[:], rhs=bias_rows[:, cols], start=True, stop=True)
+                nc.tensor.matmul(out=spread[:], lhsT=ones[:, 0:P], rhs=bias_rows[:, cols], start=True, stop=True)
                 nc.vector.tensor_copy(out=bias[:, cols], in_=spread[:])
 
         wo_grouped = keep.tile([P, PASSES, OUT_CH, PACK], BF16, align_bytes=64)
@@ -196,22 +203,27 @@ def tile_linear_retention_pb_kernel(tc, ret_w, kv_h, Wo, bo, out):
                 nc.vector.tensor_tensor(out=y[:], in0=y_ps[:], in1=bias[:, cols], op=mybir.AluOpType.add)
                 nc.sync.dma_start(out=out_dram[w, hb][:, cols], in_=y[:])
 
+        for step in range(WARM_UP):
+            keep_warm()
         for i in range(UNITS + MX_LAG):
+            prepares_wo = 1 <= i <= WO_ROUNDS
             if 0 <= i - 3 < UNITS:
                 quantise_unit(i - 3)
-            if 0 <= i - 2 < COL_HALVES:
-                quantise_wo_half(i - 2)
+            if i >= 2 and (i - 1) * WO_PER_ROUND % HALF_BLOCKS == 0 and i - 1 <= WO_ROUNDS:
+                quantise_wo_half((i - 1) * WO_PER_ROUND // HALF_BLOCKS - 1)
             if 0 <= i - 1 < UNITS:
                 read_out(i - 1, 0)
             if i < UNITS:
                 transpose_unit(i)
+            if prepares_wo:
+                transpose_wo_block((i - 1) * WO_PER_ROUND)
+                keep_warm()
             if 0 <= i - 2 < UNITS:
                 transpose_back(i - 2)
             if i == 0:
                 spread_bias()
-            if 0 <= i - 1 < COL_HALVES:
-                for cb in range((i - 1) * HALF_BLOCKS, i * HALF_BLOCKS):
-                    transpose_wo_block(cb)
+            if prepares_wo:
+                transpose_wo_block((i - 1) * WO_PER_ROUND + 1)
             if 0 <= i - 1 < UNITS:
                 read_out(i - 1, 1)
             if i >= MX_LAG:

@@ -43,16 +43,13 @@ def tile_linear_retention_pb_kernel(tc, ret_w, kv_h, Wo, bo, out):
         work = ctx.enter_context(tc.tile_pool(name="work", bufs=3))
         quantised = ctx.enter_context(tc.tile_pool(name="quantised", bufs=MX_LAG - 1))
         results = ctx.enter_context(tc.tile_pool(name="results", bufs=8))
-        psum_x = ctx.enter_context(tc.psum_pool(name="psum_x", bufs=2))
-        psum_o = ctx.enter_context(tc.psum_pool(name="psum_o", bufs=2))
-        psum_w = ctx.enter_context(tc.psum_pool(name="psum_w", bufs=2))
-        psum_y = ctx.enter_context(tc.psum_pool(name="psum_y", bufs=COL_HALVES))
+        psum = ctx.enter_context(tc.psum_pool(name="psum", bufs=8))
         ctx.enter_context(tc.manual_schedule())
 
-        bias_rows = keep.tile([P, OUT_CH], BF16)
-        nc.vector.memset(bias_rows[:], 0.0)
         ones = keep.tile([P, N_TILE], BF16)
         nc.vector.memset(ones[:], 1.0)
+        bias_rows = keep.tile([P, OUT_CH], BF16)
+        nc.vector.memset(bias_rows[:], 0.0)
         ident = keep.tile([P, P], BF16)
         make_identity(nc, ident[:])
         ident_words = keep.tile([P, P], F32)
@@ -73,7 +70,7 @@ def tile_linear_retention_pb_kernel(tc, ret_w, kv_h, Wo, bo, out):
                     nc.sync.dma_start(out=wo_sb[:, cb, :], in_=wo_dram[:, cb, :])
 
         def keep_warm():
-            unread = psum_y.tile([P, N_TILE], F32, tag="y_ps")
+            unread = psum.tile([P, N_TILE], F32, tag="bank")
             nc.tensor.matmul(out=unread[:], lhsT=ones[:, 0:P], rhs=ones[:], start=True, stop=True)
 
         bias = keep.tile([P, OUT_CH], F32)
@@ -81,7 +78,7 @@ def tile_linear_retention_pb_kernel(tc, ret_w, kv_h, Wo, bo, out):
         def spread_bias():
             for ch in range(COL_HALVES):
                 cols = slice(ch * N_TILE, (ch + 1) * N_TILE)
-                spread = psum_y.tile([P, N_TILE], F32, tag="y_ps")
+                spread = psum.tile([P, N_TILE], F32, tag="bank")
                 nc.tensor.matmul(out=spread[:], lhsT=ones[:, 0:P], rhs=bias_rows[:, cols], start=True, stop=True)
                 nc.vector.tensor_copy(out=bias[:, cols], in_=spread[:])
 
@@ -94,7 +91,7 @@ def tile_linear_retention_pb_kernel(tc, ret_w, kv_h, Wo, bo, out):
 
         def transpose_wo_block(cb):
             words = wo_sb[:, cb, :].bitcast(F32)
-            wo_t = psum_w.tile([P, PASSES, WORDS, P], F32, tag="w_ps")
+            wo_t = psum.tile([P, PASSES, WORDS, P], F32, tag="bank")
             for g in range(PASSES):
                 for u in range(WORDS):
                     first = g * P * WORDS + u
@@ -126,7 +123,7 @@ def tile_linear_retention_pb_kernel(tc, ret_w, kv_h, Wo, bo, out):
         o_scales = {}
 
         def transpose_unit(u):
-            x_t_ps = psum_x.tile([P, HEADS, P], BF16, tag="x_ps")
+            x_t_ps = psum.tile([P, HEADS, P], BF16, tag="bank")
             for n in range(HEADS):
                 nc.tensor.transpose(
                     out=x_t_ps[:, n, :], in_=x_sb[:, u, n * P : (n + 1) * P], identity=ident[:]
@@ -140,7 +137,7 @@ def tile_linear_retention_pb_kernel(tc, ret_w, kv_h, Wo, bo, out):
             if g == 0:
                 rows = work.tile([P, PASSES, WORDS, P, PAIR], BF16, tag="o_rows")
                 o_rows[u] = rows
-            o_ps = psum_o.tile([P, PACK * P], F32, tag="o_ps")
+            o_ps = psum.tile([P, PACK * P], F32, tag="bank")
             for t in range(PACK):
                 n = g * PACK + t
                 nc.tensor.matmul(
@@ -157,7 +154,7 @@ def tile_linear_retention_pb_kernel(tc, ret_w, kv_h, Wo, bo, out):
 
         def transpose_back(u):
             words = o_rows[u][:].rearrange("h g u p e -> h (g u p e)").bitcast(F32)
-            o_t_ps = psum_w.tile([P, PASSES, WORDS, P], F32, tag="w_ps")
+            o_t_ps = psum.tile([P, PASSES, WORDS, P], F32, tag="bank")
             for g in range(PASSES):
                 for v in range(WORDS):
                     first = (g * WORDS + v) * P
@@ -188,7 +185,7 @@ def tile_linear_retention_pb_kernel(tc, ret_w, kv_h, Wo, bo, out):
             w, hb = divmod(u, H_BLOCKS)
             for ch in range(COL_HALVES):
                 cols = slice(ch * N_TILE, (ch + 1) * N_TILE)
-                y_ps = psum_y.tile([P, N_TILE], F32, tag="y_ps")
+                y_ps = psum.tile([P, N_TILE], F32, tag="bank")
                 for g in range(PASSES):
                     nc.tensor.matmul_mx(
                         out=y_ps[:],

@@ -22,10 +22,11 @@ N_TILE = 512
 COL_HALVES = OUT_CH // N_TILE
 WO_BLOCKS = OUT_CH // P
 HALF_BLOCKS = N_TILE // P
-WO_PER_ROUND = 2
+WO_PER_ROUND = 1
 WO_ROUNDS = WO_BLOCKS // WO_PER_ROUND
 WARM_UP = 4
-MX_LAG = WO_ROUNDS + 2
+CHAIN = 4
+MX_START = WO_ROUNDS + 2
 
 FLOPS = 2 * HEIGHT * WIDTH * CHANNELS * HEAD_DIM + 2 * HEIGHT * WIDTH * CHANNELS * OUT_CH
 
@@ -41,7 +42,7 @@ def tile_linear_retention_pb_kernel(tc, ret_w, kv_h, Wo, bo, out):
     with ExitStack() as ctx:
         keep = ctx.enter_context(tc.tile_pool(name="keep", bufs=1))
         work = ctx.enter_context(tc.tile_pool(name="work", bufs=3))
-        quantised = ctx.enter_context(tc.tile_pool(name="quantised", bufs=MX_LAG - 1))
+        quantised = ctx.enter_context(tc.tile_pool(name="quantised", bufs=MX_START))
         results = ctx.enter_context(tc.tile_pool(name="results", bufs=8))
         psum = ctx.enter_context(tc.psum_pool(name="psum", bufs=8))
         ctx.enter_context(tc.manual_schedule())
@@ -202,26 +203,28 @@ def tile_linear_retention_pb_kernel(tc, ret_w, kv_h, Wo, bo, out):
 
         for step in range(WARM_UP):
             keep_warm()
-        for i in range(UNITS + MX_LAG):
-            prepares_wo = 1 <= i <= WO_ROUNDS
+        projected = 0
+        for i in range(UNITS + CHAIN):
             if 0 <= i - 3 < UNITS:
                 quantise_unit(i - 3)
-            if i >= 2 and (i - 1) * WO_PER_ROUND % HALF_BLOCKS == 0 and i - 1 <= WO_ROUNDS:
+            if i - 2 >= 0 and (i - 1) * WO_PER_ROUND % HALF_BLOCKS == 0 and i - 1 <= WO_ROUNDS:
                 quantise_wo_half((i - 1) * WO_PER_ROUND // HALF_BLOCKS - 1)
+            if i < MX_START and i < UNITS:
+                transpose_unit(i)
             if 0 <= i - 1 < UNITS:
                 read_out(i - 1, 0)
-            if i < UNITS:
+            if MX_START <= i < UNITS:
                 transpose_unit(i)
-            if prepares_wo:
-                transpose_wo_block((i - 1) * WO_PER_ROUND)
-                keep_warm()
-            if 0 <= i - 2 < UNITS:
-                transpose_back(i - 2)
             if i == 0:
                 spread_bias()
-            if prepares_wo:
-                transpose_wo_block((i - 1) * WO_PER_ROUND + 1)
+            for b in range(WO_PER_ROUND if 1 <= i <= WO_ROUNDS else 0):
+                transpose_wo_block((i - 1) * WO_PER_ROUND + b)
+            if 0 <= i - 2 < UNITS:
+                transpose_back(i - 2)
             if 0 <= i - 1 < UNITS:
                 read_out(i - 1, 1)
-            if i >= MX_LAG:
-                project(i - MX_LAG)
+            for step in range(2 if i >= MX_START else 0):
+                if projected <= i - CHAIN:
+                    project(projected)
+                    projected += 1
+        assert projected == UNITS

@@ -22,11 +22,11 @@ N_TILE = 512
 COL_HALVES = OUT_CH // N_TILE
 WO_BLOCKS = OUT_CH // P
 HALF_BLOCKS = N_TILE // P
-WO_PER_ROUND = 1
-WO_ROUNDS = WO_BLOCKS // WO_PER_ROUND
+WO_START = 2
 WARM_UP = 4
+LAST_BACKS = 2
 CHAIN = 4
-MX_START = WO_ROUNDS + 2
+MX_START = WO_START + WO_BLOCKS + 1
 
 FLOPS = 2 * HEIGHT * WIDTH * CHANNELS * HEAD_DIM + 2 * HEIGHT * WIDTH * CHANNELS * OUT_CH
 
@@ -66,9 +66,8 @@ def tile_linear_retention_pb_kernel(tc, ret_w, kv_h, Wo, bo, out):
                 nc.sync.dma_start(out=kv_sb[:, w], in_=kv_dram[w])
             if u == 0:
                 nc.sync.dma_start(out=bias_rows[0:1, :], in_=bo.rearrange("(o c) -> o c", o=1))
-            if 1 <= u <= WO_ROUNDS:
-                for cb in range((u - 1) * WO_PER_ROUND, u * WO_PER_ROUND):
-                    nc.sync.dma_start(out=wo_sb[:, cb, :], in_=wo_dram[:, cb, :])
+            if 1 <= u <= WO_BLOCKS:
+                nc.sync.dma_start(out=wo_sb[:, u - 1, :], in_=wo_dram[:, u - 1, :])
 
         def keep_warm():
             unread = psum.tile([P, N_TILE], F32, tag="bank")
@@ -90,23 +89,24 @@ def tile_linear_retention_pb_kernel(tc, ret_w, kv_h, Wo, bo, out):
         wo_codes = keep.tile([P, PASSES, OUT_CH], U32, align_bytes=64)
         wo_scales = keep.tile([P, PASSES, OUT_CH], U8, align_bytes=64)
 
+        wo_split = keep.tile([P, WO_BLOCKS, PASSES, WORDS, P], F32)
+
+        def split_wo_block(cb):
+            nc.vector.tensor_copy(
+                out=wo_split[:, cb],
+                in_=wo_sb[:, cb, :].bitcast(F32).rearrange("c (g p u) -> c g u p", g=PASSES, u=WORDS),
+            )
+
         def transpose_wo_block(cb):
-            words = wo_sb[:, cb, :].bitcast(F32)
             wo_t = psum.tile([P, PASSES, WORDS, P], F32, tag="bank")
             for g in range(PASSES):
                 for u in range(WORDS):
-                    first = g * P * WORDS + u
                     nc.tensor.transpose(
-                        out=wo_t[:, g, u, :],
-                        in_=words[:, first : first + P * WORDS - u : WORDS],
-                        identity=ident_words[:],
+                        out=wo_t[:, g, u, :], in_=wo_split[:, cb, g, u, :], identity=ident_words[:]
                     )
             grouped_block = wo_grouped_words[:, :, cb * P : (cb + 1) * P, :]
             hopping = wo_t[:].rearrange("p g u c -> p g c u")
-            if cb % 2 == 0:
-                nc.vector.tensor_copy(out=grouped_block, in_=hopping)
-            else:
-                nc.scalar.copy(out=grouped_block, in_=hopping)
+            nc.vector.tensor_copy(out=grouped_block, in_=hopping)
 
         def quantise_wo_half(ch):
             cols = slice(ch * N_TILE, (ch + 1) * N_TILE)
@@ -163,12 +163,14 @@ def tile_linear_retention_pb_kernel(tc, ret_w, kv_h, Wo, bo, out):
                         out=o_t_ps[:, g, v, :], in_=words[:, first : first + P], identity=ident_words[:]
                     )
             grouped = work.tile([P, PASSES, P, PACK], BF16, tag="o_grouped", align_bytes=64)
-            nc.vector.tensor_copy(
-                out=grouped[:].rearrange("p g h t -> p (g h t)").bitcast(F32).rearrange(
-                    "p (g h u) -> p g h u", g=PASSES, u=WORDS
-                ),
-                in_=o_t_ps[:].rearrange("p g u h -> p g h u"),
+            grouped_words = grouped[:].rearrange("p g h t -> p (g h t)").bitcast(F32).rearrange(
+                "p (g h u) -> p g h u", g=PASSES, u=WORDS
             )
+            hopping = o_t_ps[:].rearrange("p g u h -> p g h u")
+            if u < UNITS - LAST_BACKS:
+                nc.vector.tensor_copy(out=grouped_words, in_=hopping)
+            else:
+                nc.scalar.copy(out=grouped_words, in_=hopping)
             o_grouped[u] = grouped
 
         def quantise_unit(u):
@@ -205,26 +207,35 @@ def tile_linear_retention_pb_kernel(tc, ret_w, kv_h, Wo, bo, out):
             keep_warm()
         projected = 0
         for i in range(UNITS + CHAIN):
+            if 0 <= i - WO_START + 1 < WO_BLOCKS:
+                split_wo_block(i - WO_START + 1)
             if 0 <= i - 3 < UNITS:
                 quantise_unit(i - 3)
-            if i - 2 >= 0 and (i - 1) * WO_PER_ROUND % HALF_BLOCKS == 0 and i - 1 <= WO_ROUNDS:
-                quantise_wo_half((i - 1) * WO_PER_ROUND // HALF_BLOCKS - 1)
-            if i < MX_START and i < UNITS:
-                transpose_unit(i)
-            if 0 <= i - 1 < UNITS:
-                read_out(i - 1, 0)
-            if MX_START <= i < UNITS:
-                transpose_unit(i)
-            if i == 0:
-                spread_bias()
-            for b in range(WO_PER_ROUND if 1 <= i <= WO_ROUNDS else 0):
-                transpose_wo_block((i - 1) * WO_PER_ROUND + b)
-            if 0 <= i - 2 < UNITS:
-                transpose_back(i - 2)
-            if 0 <= i - 1 < UNITS:
-                read_out(i - 1, 1)
-            for step in range(2 if i >= MX_START else 0):
-                if projected <= i - CHAIN:
-                    project(projected)
-                    projected += 1
+            if i - WO_START - 1 >= 0 and (i - WO_START) % HALF_BLOCKS == 0 and i - WO_START <= WO_BLOCKS:
+                quantise_wo_half((i - WO_START) // HALF_BLOCKS - 1)
+            if i < MX_START:
+                if i < UNITS:
+                    transpose_unit(i)
+                if i == 0:
+                    spread_bias()
+                if 0 <= i - 1 < UNITS:
+                    read_out(i - 1, 0)
+                    read_out(i - 1, 1)
+                if 0 <= i - WO_START < WO_BLOCKS:
+                    transpose_wo_block(i - WO_START)
+                if 0 <= i - 2 < UNITS:
+                    transpose_back(i - 2)
+            else:
+                if 0 <= i - 1 < UNITS:
+                    read_out(i - 1, 0)
+                if i < UNITS:
+                    transpose_unit(i)
+                if 0 <= i - 2 < UNITS:
+                    transpose_back(i - 2)
+                if 0 <= i - 1 < UNITS:
+                    read_out(i - 1, 1)
+                for step in range(2):
+                    if projected <= i - CHAIN:
+                        project(projected)
+                        projected += 1
         assert projected == UNITS

@@ -24,7 +24,7 @@ WO_BLOCKS = OUT_CH // P
 HALF_BLOCKS = N_TILE // P
 WO_START = 2
 WARM_UP = 4
-LAST_BACKS = 2
+LAST_BACKS = 8
 CHAIN = 4
 MX_START = WO_START + WO_BLOCKS + 1
 
@@ -106,7 +106,10 @@ def tile_linear_retention_pb_kernel(tc, ret_w, kv_h, Wo, bo, out):
                     )
             grouped_block = wo_grouped_words[:, :, cb * P : (cb + 1) * P, :]
             hopping = wo_t[:].rearrange("p g u c -> p g c u")
-            nc.vector.tensor_copy(out=grouped_block, in_=hopping)
+            if cb % 2 == 0:
+                nc.vector.tensor_copy(out=grouped_block, in_=hopping)
+            else:
+                nc.scalar.copy(out=grouped_block, in_=hopping)
 
         def quantise_wo_half(ch):
             cols = slice(ch * N_TILE, (ch + 1) * N_TILE)
@@ -118,7 +121,8 @@ def tile_linear_retention_pb_kernel(tc, ret_w, kv_h, Wo, bo, out):
                 )
 
         x_t = {}
-        o_rows = {}
+        o_banks = {}
+        o_words = {}
         o_grouped = {}
         o_codes = {}
         o_scales = {}
@@ -136,31 +140,33 @@ def tile_linear_retention_pb_kernel(tc, ret_w, kv_h, Wo, bo, out):
         def read_out(u, g):
             w = u // H_BLOCKS
             if g == 0:
-                rows = work.tile([P, PASSES, WORDS, P, PAIR], BF16, tag="o_rows")
-                o_rows[u] = rows
-            o_ps = psum.tile([P, PACK * P], F32, tag="bank")
+                o_bank = psum.tile([P, PASSES, PACK * P], BF16, tag="bank")
+                o_banks[u] = o_bank
             for t in range(PACK):
                 n = g * PACK + t
                 nc.tensor.matmul(
-                    out=o_ps[:, t * P : (t + 1) * P],
+                    out=o_banks[u][:, g, t * P : (t + 1) * P],
                     lhsT=x_t[u][:, n, :],
                     rhs=kv_sb[:, w, n, :],
                     start=True,
                     stop=True,
                 )
-            nc.scalar.copy(
-                out=o_rows[u][:, g],
-                in_=o_ps[:].rearrange("h (p u e) -> h u p e", u=WORDS, e=PAIR),
-            )
+            if g == PASSES - 1:
+                words = work.tile([P, PASSES, WORDS, P], F32, tag="o_words")
+                nc.scalar.copy(
+                    out=words[:],
+                    in_=o_banks[u][:].rearrange("h g k -> h (g k)").bitcast(F32).rearrange(
+                        "h (g p u) -> h g u p", g=PASSES, u=WORDS
+                    ),
+                )
+                o_words[u] = words
 
         def transpose_back(u):
-            words = o_rows[u][:].rearrange("h g u p e -> h (g u p e)").bitcast(F32)
             o_t_ps = psum.tile([P, PASSES, WORDS, P], F32, tag="bank")
             for g in range(PASSES):
                 for v in range(WORDS):
-                    first = (g * WORDS + v) * P
                     nc.tensor.transpose(
-                        out=o_t_ps[:, g, v, :], in_=words[:, first : first + P], identity=ident_words[:]
+                        out=o_t_ps[:, g, v, :], in_=o_words[u][:, g, v, :], identity=ident_words[:]
                     )
             grouped = work.tile([P, PASSES, P, PACK], BF16, tag="o_grouped", align_bytes=64)
             grouped_words = grouped[:].rearrange("p g h t -> p (g h t)").bitcast(F32).rearrange(

from contextlib import ExitStack

import concourse.mybir as mybir
from concourse.masks import make_identity

BF16 = mybir.dt.bfloat16
F32 = mybir.dt.float32
U32 = mybir.dt.uint32
U8 = mybir.dt.uint8
FP8X4 = mybir.dt.float8_e4m3fn_x4

P = 128
HEIGHT, WIDTH, HEADS, HEAD_DIM, OUT_CH = 512, 4, 8, 128, 1024
CHANNELS = HEADS * HEAD_DIM
PACK = 4
PASSES = CHANNELS // (P * PACK)
PAIR = 2
WORDS = PACK // PAIR
H_BLOCKS = HEIGHT // P
UNITS = WIDTH * H_BLOCKS
N_TILE = 512
COL_HALVES = OUT_CH // N_TILE
WO_BLOCKS = OUT_CH // P
HALF_BLOCKS = N_TILE // P
WO_START = 2
WARM_UP = 4
LAST_BACKS = 8
CHAIN = 4
MX_START = WO_START + WO_BLOCKS + 1

FLOPS = 2 * HEIGHT * WIDTH * CHANNELS * HEAD_DIM + 2 * HEIGHT * WIDTH * CHANNELS * OUT_CH


def tile_linear_retention_pb_kernel(tc, ret_w, kv_h, Wo, bo, out):
    nc = tc.nc

    x_dram = ret_w[0].rearrange("(hb h) w n e -> w hb h (n e)", h=P)
    kv_dram = kv_h[0].rearrange("w n e f -> w e n f")
    wo_dram = Wo.rearrange("(cb c) k -> c cb k", c=P)
    out_dram = out[0].rearrange("(hb h w) c -> w hb h c", h=P, w=WIDTH)

    with ExitStack() as ctx:
        keep = ctx.enter_context(tc.tile_pool(name="keep", bufs=1))
        work = ctx.enter_context(tc.tile_pool(name="work", bufs=3))
        quantised = ctx.enter_context(tc.tile_pool(name="quantised", bufs=MX_START))
        results = ctx.enter_context(tc.tile_pool(name="results", bufs=8))
        psum = ctx.enter_context(tc.psum_pool(name="psum", bufs=8))
        ctx.enter_context(tc.manual_schedule())

        ones = keep.tile([P, N_TILE], BF16)
        nc.vector.memset(ones[:], 1.0)
        bias_rows = keep.tile([P, OUT_CH], BF16)
        nc.vector.memset(bias_rows[:], 0.0)
        ident = keep.tile([P, P], BF16)
        make_identity(nc, ident[:])
        ident_words = keep.tile([P, P], F32)
        make_identity(nc, ident_words[:])

        x_sb = keep.tile([P, UNITS, CHANNELS], BF16)
        kv_sb = keep.tile([P, WIDTH, HEADS, HEAD_DIM], BF16)
        wo_sb = keep.tile([P, WO_BLOCKS, CHANNELS], BF16)
        for u in range(UNITS):
            w, hb = divmod(u, H_BLOCKS)
            nc.sync.dma_start(out=x_sb[:, u, :], in_=x_dram[w, hb])
            if hb == 0:
                nc.sync.dma_start(out=kv_sb[:, w], in_=kv_dram[w])
            if u == 0:
                nc.sync.dma_start(out=bias_rows[0:1, :], in_=bo.rearrange("(o c) -> o c", o=1))
            if 1 <= u <= WO_BLOCKS:
                nc.sync.dma_start(out=wo_sb[:, u - 1, :], in_=wo_dram[:, u - 1, :])

        def keep_warm():
            unread = psum.tile([P, N_TILE], F32, tag="bank")
            nc.tensor.matmul(out=unread[:], lhsT=ones[:, 0:P], rhs=ones[:], start=True, stop=True)

        bias = keep.tile([P, OUT_CH], F32)

        def spread_bias():
            for ch in range(COL_HALVES):
                cols = slice(ch * N_TILE, (ch + 1) * N_TILE)
                spread = psum.tile([P, N_TILE], F32, tag="bank")
                nc.tensor.matmul(out=spread[:], lhsT=ones[:, 0:P], rhs=bias_rows[:, cols], start=True, stop=True)
                nc.vector.tensor_copy(out=bias[:, cols], in_=spread[:])

        wo_grouped = keep.tile([P, PASSES, OUT_CH, PACK], BF16, align_bytes=64)
        wo_grouped_words = wo_grouped[:].rearrange("p g c t -> p (g c t)").bitcast(F32).rearrange(
            "p (g c u) -> p g c u", g=PASSES, u=WORDS
        )
        wo_codes = keep.tile([P, PASSES, OUT_CH], U32, align_bytes=64)
        wo_scales = keep.tile([P, PASSES, OUT_CH], U8, align_bytes=64)

        wo_split = keep.tile([P, WO_BLOCKS, PASSES, WORDS, P], F32)

        def split_wo_block(cb):
            nc.vector.tensor_copy(
                out=wo_split[:, cb],
                in_=wo_sb[:, cb, :].bitcast(F32).rearrange("c (g p u) -> c g u p", g=PASSES, u=WORDS),
            )

        def transpose_wo_block(cb):
            wo_t = psum.tile([P, PASSES, WORDS, P], F32, tag="bank")
            for g in range(PASSES):
                for u in range(WORDS):
                    nc.tensor.transpose(
                        out=wo_t[:, g, u, :], in_=wo_split[:, cb, g, u, :], identity=ident_words[:]
                    )
            grouped_block = wo_grouped_words[:, :, cb * P : (cb + 1) * P, :]
            hopping = wo_t[:].rearrange("p g u c -> p g c u")
            if cb % 2 == 0:
                nc.vector.tensor_copy(out=grouped_block, in_=hopping)
            else:
                nc.scalar.copy(out=grouped_block, in_=hopping)

        def quantise_wo_half(ch):
            cols = slice(ch * N_TILE, (ch + 1) * N_TILE)
            for g in range(PASSES):
                nc.vector.quantize_mx(
                    out=wo_codes[:, g, cols].bitcast(FP8X4),
                    scales=wo_scales[:, g, cols],
                    in_=wo_grouped[:, g, cols, :].rearrange("p c t -> p (c t)"),
                )

        x_t = {}
        o_banks = {}
        o_words = {}
        o_grouped = {}
        o_codes = {}
        o_scales = {}

        def transpose_unit(u):
            x_t_ps = psum.tile([P, HEADS, P], BF16, tag="bank")
            for n in range(HEADS):
                nc.tensor.transpose(
                    out=x_t_ps[:, n, :], in_=x_sb[:, u, n * P : (n + 1) * P], identity=ident[:]
                )
            x_t_sb = work.tile([P, HEADS, P], BF16, tag="x_t")
            nc.scalar.copy(out=x_t_sb[:], in_=x_t_ps[:])
            x_t[u] = x_t_sb

        def read_out(u, g):
            w = u // H_BLOCKS
            if g == 0:
                o_bank = psum.tile([P, PASSES, PACK * P], BF16, tag="bank")
                o_banks[u] = o_bank
            for t in range(PACK):
                n = g * PACK + t
                nc.tensor.matmul(
                    out=o_banks[u][:, g, t * P : (t + 1) * P],
                    lhsT=x_t[u][:, n, :],
                    rhs=kv_sb[:, w, n, :],
                    start=True,
                    stop=True,
                )
            if g == PASSES - 1:
                words = work.tile([P, PASSES, WORDS, P], F32, tag="o_words")
                nc.scalar.copy(
                    out=words[:],
                    in_=o_banks[u][:].rearrange("h g k -> h (g k)").bitcast(F32).rearrange(
                        "h (g p u) -> h g u p", g=PASSES, u=WORDS
                    ),
                )
                o_words[u] = words

        def transpose_back(u):
            o_t_ps = psum.tile([P, PASSES, WORDS, P], F32, tag="bank")
            for g in range(PASSES):
                for v in range(WORDS):
                    nc.tensor.transpose(
                        out=o_t_ps[:, g, v, :], in_=o_words[u][:, g, v, :], identity=ident_words[:]
                    )
            grouped = work.tile([P, PASSES, P, PACK], BF16, tag="o_grouped", align_bytes=64)
            grouped_words = grouped[:].rearrange("p g h t -> p (g h t)").bitcast(F32).rearrange(
                "p (g h u) -> p g h u", g=PASSES, u=WORDS
            )
            hopping = o_t_ps[:].rearrange("p g u h -> p g h u")
            if u < UNITS - LAST_BACKS:
                nc.vector.tensor_copy(out=grouped_words, in_=hopping)
            else:
                nc.scalar.copy(out=grouped_words, in_=hopping)
            o_grouped[u] = grouped

        def quantise_unit(u):
            codes = quantised.tile([P, PASSES, P], U32, tag="o_codes", align_bytes=64)
            scales = quantised.tile([P, PASSES, P], U8, tag="o_scales", align_bytes=64)
            nc.vector.quantize_mx(
                out=codes[:].rearrange("p g h -> p (g h)").bitcast(FP8X4),
                scales=scales[:].rearrange("p g h -> p (g h)"),
                in_=o_grouped[u][:].rearrange("p g h t -> p (g h t)"),
            )
            o_codes[u] = codes
            o_scales[u] = scales

        def project(u):
            w, hb = divmod(u, H_BLOCKS)
            for ch in range(COL_HALVES):
                cols = slice(ch * N_TILE, (ch + 1) * N_TILE)
                y_ps = psum.tile([P, N_TILE], F32, tag="bank")
                for g in range(PASSES):
                    nc.tensor.matmul_mx(
                        out=y_ps[:],
                        lhsT=o_codes[u][:, g, :].bitcast(FP8X4),
                        lhsT_scale=o_scales[u][:, g, :],
                        rhs=wo_codes[:, g, cols].bitcast(FP8X4),
                        rhs_scale=wo_scales[:, g, cols],
                        start=(g == 0),
                        stop=(g == PASSES - 1),
                    )
                y = results.tile([P, N_TILE], F32, tag="y")
                nc.vector.tensor_tensor(out=y[:], in0=y_ps[:], in1=bias[:, cols], op=mybir.AluOpType.add)
                nc.sync.dma_start(out=out_dram[w, hb][:, cols], in_=y[:])

        for step in range(WARM_UP):
            keep_warm()
        projected = 0
        for i in range(UNITS + CHAIN):
            if 0 <= i - WO_START + 1 < WO_BLOCKS:
                split_wo_block(i - WO_START + 1)
            if 0 <= i - 3 < UNITS:
                quantise_unit(i - 3)
            if i - WO_START - 1 >= 0 and (i - WO_START) % HALF_BLOCKS == 0 and i - WO_START <= WO_BLOCKS:
                quantise_wo_half((i - WO_START) // HALF_BLOCKS - 1)
            if i < MX_START:
                if i < UNITS:
                    transpose_unit(i)
                if i == 0:
                    spread_bias()
                if 0 <= i - 1 < UNITS:
                    read_out(i - 1, 0)
                    read_out(i - 1, 1)
                if 0 <= i - WO_START < WO_BLOCKS:
                    transpose_wo_block(i - WO_START)
                if 0 <= i - 2 < UNITS:
                    transpose_back(i - 2)
            else:
                if 0 <= i - 1 < UNITS:
                    read_out(i - 1, 0)
                if i < UNITS:
                    transpose_unit(i)
                if 0 <= i - 2 < UNITS:
                    transpose_back(i - 2)
                if 0 <= i - 1 < UNITS:
                    read_out(i - 1, 1)
                for step in range(2):
                    if projected <= i - CHAIN:
                        project(projected)
                        projected += 1
        assert projected == UNITS
